import numpy as np
import ml_dtypes


def mxq(x, axis, fmt="e4m3"):
    dtype, down = {"e4m3": (ml_dtypes.float8_e4m3fn, 7), "e5m2": (ml_dtypes.float8_e5m2, 14)}[fmt]
    v = np.moveaxis(np.asarray(x, np.float32).astype(ml_dtypes.bfloat16).astype(np.float64), axis, -1)
    blocks = v.reshape(v.shape[:-1] + (-1, 32))
    amax = np.abs(blocks).max(-1, keepdims=True)
    byte = np.maximum(np.where(amax > 0, np.frexp(amax)[1] - 1 + 127, 0) - down, 1)
    scale = np.exp2(byte - 127.0)
    codes = (blocks / scale).astype(np.float32).astype(dtype).astype(np.float64)
    return np.moveaxis((codes * scale).reshape(v.shape), -1, axis)


WIDE = False


def mx_kscale(k):
    if not WIDE:
        return np.ones(k)
    levels = np.array([18, -18])
    if k % 512:
        return np.exp2(np.random.permutation(np.resize(levels, k // 32))).repeat(32)
    a = np.empty((k // 512, 16))
    for p in range(k // 512):
        a[p, :8] = np.random.permutation(np.resize(levels, 8))
        for g in range(8):
            far = levels[np.abs(levels - a[p, g]) >= 10]
            a[p, g + 8] = far[np.random.randint(len(far))]
    return np.exp2(a.ravel()).repeat(32)


BF16 = ml_dtypes.bfloat16


def bf(x):
    return np.asarray(x, np.float32).astype(BF16)


def f64(x):
    return np.asarray(x).astype(np.float64)


B, T, H, KV, HD = 1, 1024, 8, 2, 128
D = H * HD
KVD = KV * HD
O = D + 2 * KVD
ROPE_BASE = 500000.0
CLAMP = 8.0


def rope_tables():
    inv = 1.0 / ROPE_BASE ** (np.arange(0, HD, 2) / HD)
    freqs = np.arange(T)[:, None] * inv[None, :]
    return np.cos(freqs)[None, None], np.sin(freqs)[None, None]


def rope(u):
    n = u.shape[1]
    cos, sin = rope_tables()
    p = u.reshape(B, n, T, HD // 2, 2)
    a, b = p[..., 0], p[..., 1]
    return np.stack([a * cos - b * sin, a * sin + b * cos], axis=-1).reshape(B, n, T, HD)


def rope_back(g):
    n = g.shape[1]
    cos, sin = rope_tables()
    p = g.reshape(B, n, T, HD // 2, 2)
    a, b = p[..., 0], p[..., 1]
    return np.stack([a * cos + b * sin, b * cos - a * sin], axis=-1).reshape(B, n, T, HD)


def split_heads(y, n):
    return y.reshape(B, T, n, HD).transpose(0, 2, 1, 3)


def join_heads(y):
    return y.transpose(0, 2, 1, 3).reshape(B * T, y.shape[1] * HD)


def clip_back(g, z):
    return np.where(np.abs(z) < CLAMP, g, 0.0)


def draw_grad(z, u, s):
    n = z.shape[1]
    g = np.random.standard_normal((B, n, T, HD)) * np.exp2(np.random.randint(-6, 1, (B, 1, T, 1)))
    g = np.where(np.abs(np.abs(z) - CLAMP) > 0.004, g, 0.0)
    return bf(g * u.reshape(1, n, 1, HD) / s.reshape(1, 1, T, 1))


def setup_inputs():
    s = mx_kscale(T)
    u = mx_kscale(O)
    x0 = bf(np.random.standard_normal((B, T, D)))
    w0 = bf(np.random.standard_normal((O, D)) * 0.5 * CLAMP / np.sqrt(D))
    qkv = f64(x0) @ f64(w0).T
    q_rot = rope(split_heads(qkv[..., :D], H))
    k_rot = rope(split_heads(qkv[..., D:D + KVD], KV))
    v_pre = split_heads(qkv[..., D + KVD:], KV)
    g0 = draw_grad(q_rot, u[:D], s)
    g1 = draw_grad(k_rot, u[D:D + KVD], s)
    g2 = draw_grad(v_pre, u[D + KVD:], s)
    return {"x": bf(f64(x0) * s[None, :, None]),
            "w_qkv": bf(f64(w0) / u[:, None]),
            "q_rot": np.asarray(q_rot, np.float32),
            "k_rot": np.asarray(k_rot, np.float32),
            "v_pre": np.asarray(v_pre, np.float32),
            "grad_0": g0, "grad_1": g1, "grad_2": g2}


def reference(x, w_qkv, q_rot, k_rot, v_pre, grad_0, grad_1, grad_2):
    dq = rope_back(clip_back(f64(grad_0), f64(q_rot)))
    dk = rope_back(clip_back(f64(grad_1), f64(k_rot)))
    dv = clip_back(f64(grad_2), f64(v_pre))
    dqkv = np.concatenate([join_heads(dq), join_heads(dk), join_heads(dv)], axis=1)
    xf = f64(x).reshape(B * T, D)
    dx = mxq(dqkv, 1, "e5m2") @ mxq(f64(w_qkv), 0, "e4m3")
    dw = mxq(dqkv, 0, "e5m2").T @ mxq(xf, 0, "e4m3")
    return dx.reshape(B, T, D), dw

@@ -1,0 +1,374 @@
+import math
+from contextlib import ExitStack
+
+import concourse.mybir as mybir
+from concourse.masks import make_identity
+
+T, D, O = 1024, 1024, 1536
+HD = 128
+ROPE_BASE = 500000.0
+CLAMP = 8.0
+FLOPS = 2 * 2 * T * D * O
+
+F32 = mybir.dt.float32
+BF16 = mybir.dt.bfloat16
+I32 = mybir.dt.int32
+U32 = mybir.dt.uint32
+U8 = mybir.dt.uint8
+E4M3 = mybir.dt.float8_e4m3fn_x4
+E5M2 = mybir.dt.float8_e5m2_x4
+ALU = mybir.AluOpType
+ACT = mybir.ActivationFunctionType
+
+P = 128
+
+
+def tile_dbrxattention_pa_v_kernel(
+    tc, x, w_qkv, q_rot, k_rot, v_pre, grad_0, grad_1, grad_2, out_0, out_1
+):
+    nc = tc.nc
+    with ExitStack() as ctx:
+        const = ctx.enter_context(tc.tile_pool(name="const", bufs=1))
+        keep = ctx.enter_context(tc.tile_pool(name="keep", bufs=1))
+        pq = ctx.enter_context(tc.tile_pool(name="pq", bufs=6))
+        pg = ctx.enter_context(tc.tile_pool(name="pg", bufs=8))
+        praw = ctx.enter_context(tc.tile_pool(name="praw", bufs=3))
+        work = ctx.enter_context(tc.tile_pool(name="work", bufs=3))
+        pst = ctx.enter_context(tc.tile_pool(name="pst", bufs=4))
+        ptp = ctx.enter_context(tc.psum_pool(name="ptp", bufs=3))
+        pacc = ctx.enter_context(tc.psum_pool(name="pacc", bufs=5))
+        ctx.enter_context(tc.manual_schedule())
+
+        qt = {}
+        gt = {}
+        raw = {}
+
+        def load_unit(u):
+            g, pr = divmod(u, 6)
+            rows = slice(512 * g, 512 * g + 512)
+            if pr < 4:
+                sv = q_rot[0, 2 * pr : 2 * pr + 2, rows, :]
+                gr = grad_0[0, 2 * pr : 2 * pr + 2, rows, :]
+            elif pr == 4:
+                sv = k_rot[0, :, rows, :]
+                gr = grad_1[0, :, rows, :]
+            else:
+                sv = v_pre[0, :, rows, :]
+                gr = grad_2[0, :, rows, :]
+            q_t = pq.tile([P, 2, 512], F32, name="q_t")
+            nc.sync.dma_start(out=q_t[:], in_=sv.rearrange("h (p j) c -> p h (j c)", j=4))
+            g_t = pg.tile([P, 2, 512], BF16, name="g_t")
+            nc.sync.dma_start(out=g_t[:], in_=gr.rearrange("h (p j) c -> p h (j c)", j=4))
+            qt[u] = q_t
+            gt[u] = g_t
+
+        def load_w(i):
+            r = praw.tile([P, 4, 1024], BF16, name="raw_t")
+            nc.sync.dma_start(
+                out=r[:], in_=w_qkv[512 * i : 512 * i + 512, :].rearrange("(p j) d -> p j d", j=4)
+            )
+            raw["w", i] = r
+
+        def load_x(i):
+            r = praw.tile([P, 4, 1024], BF16, name="raw_t")
+            nc.sync.dma_start(
+                out=r[:], in_=x[0, 512 * i : 512 * i + 512, :].rearrange("(p j) d -> p j d", j=4)
+            )
+            raw["x", i] = r
+
+        tok = const.tile([P, 8], F32, name="tok")
+        nc.gpsimd.iota(
+            tok[:].rearrange("p (g j) -> p g j", j=4),
+            [[512, 2], [1, 4]],
+            base=0,
+            channel_multiplier=4,
+            allow_small_or_imprecise_dtypes=True,
+        )
+        ident = const.tile([P, P], BF16, name="ident")
+        make_identity(nc, ident[:])
+        sgn = const.tile([P, 2], F32, name="sgn")
+        nc.vector.memset(sgn[:, 0:1], 1.0)
+        nc.vector.memset(sgn[:, 1:2], -1.0)
+        warm = const.tile([P, 1], F32, name="warm")
+        nc.scalar.activation(warm[:], sgn[:, 0:1], ACT.Sin)
+
+        load_unit(0)
+        load_unit(1)
+        load_w(0)
+        load_unit(2)
+        load_unit(3)
+        load_w(1)
+        load_unit(4)
+        load_unit(5)
+
+        y = const.tile([P, 8, 64], F32, name="y")
+        for i in range(64):
+            c = ROPE_BASE ** (-2.0 * i / HD) / (2.0 * math.pi)
+            if i % 5 < 3:
+                nc.vector.tensor_scalar_mul(y[:, :, i], tok[:], c)
+            else:
+                nc.scalar.activation(y[:, :, i], tok[:], ACT.Copy, scale=c)
+        n_i = const.tile([P, 8, 64], I32, name="n_i")
+        nc.vector.tensor_copy(out=n_i[:], in_=y[:])
+        f = const.tile([P, 8, 64], F32, name="f")
+        nc.vector.tensor_tensor(out=f[:], in0=y[:], in1=n_i[:], op=ALU.subtract)
+        fa = const.tile([P, 8, 64], F32, name="fa")
+        nc.scalar.activation(fa[:], f[:], ACT.Abs)
+        f2 = const.tile([P, 8, 64, 2], F32, name="f2")
+        nc.vector.tensor_tensor(
+            out=f2[:],
+            in0=f[:].unsqueeze(3).to_broadcast([P, 8, 64, 2]),
+            in1=sgn[:].unsqueeze(1).unsqueeze(1).to_broadcast([P, 8, 64, 2]),
+            op=ALU.mult,
+        )
+        fc = const.tile([P, 8, 64], F32, name="fc")
+        nc.vector.tensor_scalar(
+            out=fc[:], in0=fa[:], scalar1=-1.0, scalar2=0.25, op0=ALU.mult, op1=ALU.add
+        )
+        cos_t = []
+        sin_t = []
+        for g in range(2):
+            cg = const.tile([P, 4, 64, 2], F32, name=f"cos{g}")
+            cos_t.append(cg)
+            sg = const.tile([P, 4, 64, 2], F32, name=f"sin{g}")
+            sin_t.append(sg)
+
+        def trig(g):
+            js = slice(4 * g, 4 * g + 4)
+            nc.scalar.activation(
+                cos_t[g][:],
+                fc[:, js, :].unsqueeze(3).to_broadcast([P, 4, 64, 2]),
+                ACT.Sin,
+                scale=2.0 * math.pi,
+            )
+            nc.scalar.activation(sin_t[g][:], f2[:, js, :, :], ACT.Sin, scale=2.0 * math.pi)
+
+        ha = {}
+        mk = {}
+        gm = {}
+        t1 = {}
+        t2 = {}
+        dq = {}
+
+        def step_abs(u):
+            a = work.tile([P, 1024], BF16, name="ha_t")
+            top = (
+                qt[u][:]
+                .rearrange("p h n -> p (h n)")
+                .bitcast(BF16)
+                .rearrange("p (n e) -> p n e", e=2)[:, :, 1]
+            )
+            nc.scalar.activation(a[:], top, ACT.Abs)
+            ha[u] = a
+
+        def step_cmp(u):
+            m = work.tile([P, 1024], BF16, name="mk_t")
+            nc.vector.tensor_scalar(
+                out=m[:], in0=ha[u][:], scalar1=CLAMP, scalar2=None, op0=ALU.is_lt
+            )
+            mk[u] = m
+
+        def new_dq(k):
+            d_t = work.tile([P, 4, P, 4], BF16, name="dq_t", align_bytes=64)
+            dq[k] = d_t
+
+        def step_mask(u):
+            k, s = divmod(u, 2)
+            if u % 6 == 5:
+                for h in range(2):
+                    nc.vector.tensor_tensor(
+                        out=dq[k][:, :, 64 + 32 * h : 96 + 32 * h, :].rearrange("p t q j -> p q j t"),
+                        in0=mk[u][:, 512 * h : 512 * h + 512].rearrange("p (j q t) -> p q j t", j=4, t=4),
+                        in1=gt[u][:, h, :].rearrange("p (j q t) -> p q j t", j=4, t=4),
+                        op=ALU.mult,
+                    )
+            else:
+                g_m = work.tile([P, 2, 4, 64, 2], BF16, name="gm_t")
+                nc.vector.tensor_tensor(
+                    out=g_m[:].rearrange("p h j i e -> p (h j i e)"),
+                    in0=mk[u][:],
+                    in1=gt[u][:].rearrange("p h n -> p (h n)"),
+                    op=ALU.mult,
+                )
+                gm[u] = g_m
+
+        def step_cos(u):
+            a = work.tile([P, 4, 2, P], F32, name="t1_t")
+            nc.vector.tensor_tensor(
+                out=a[:].rearrange("p j h c -> p h j c"),
+                in0=gm[u][:].rearrange("p h j i e -> p h j (i e)"),
+                in1=cos_t[u // 6][:].rearrange("p j i e -> p j (i e)").unsqueeze(1).to_broadcast([P, 2, 4, P]),
+                op=ALU.mult,
+            )
+            t1[u] = a
+
+        def step_sin(u):
+            a = work.tile([P, 4, 2, P], F32, name="t2_t")
+            nc.vector.tensor_tensor(
+                out=a[:].rearrange("p j h (i e) -> p h j i e", e=2),
+                in0=gm[u][:, :, :, :, ::-1],
+                in1=sin_t[u // 6][:].unsqueeze(1).to_broadcast([P, 2, 4, 64, 2]),
+                op=ALU.mult,
+            )
+            t2[u] = a
+
+        def step_add(u):
+            k, s = divmod(u, 2)
+            nc.vector.tensor_tensor(
+                out=dq[k][:, :, 64 * s : 64 * s + 64, :].rearrange("p t q j -> p q j t"),
+                in0=t1[u][:].rearrange("p j h (q t) -> p (h q) j t", t=4),
+                in1=t2[u][:].rearrange("p j h (q t) -> p (h q) j t", t=4),
+                op=ALU.add,
+            )
+
+        tokc = {}
+        toks = {}
+        featc = {}
+        feats = {}
+
+        def quant_tok(k):
+            c = keep.tile([P, 512], U32, name=f"tokc{k}", align_bytes=64)
+            s = keep.tile([P, 512], U8, name=f"toks{k}", align_bytes=64)
+            nc.vector.quantize_mx(
+                out=c[:].bitcast(E5M2), scales=s[:], in_=dq[k][:].rearrange("p t q j -> p (t q j)")
+            )
+            tokc[k] = c
+            toks[k] = s
+
+        dqt = {}
+
+        def transposes(k):
+            o = work.tile([P, 4, P, 4], BF16, name="dqt_t", align_bytes=64)
+            for j in range(4):
+                tp = ptp.tile([P, 4, P], BF16, name="tp_t")
+                for t in range(4):
+                    nc.tensor.transpose(tp[:, t, :], dq[k][:, t, :, j], ident[:])
+                nc.scalar.copy(out=o[:, j], in_=tp[:].rearrange("p t n -> p n t"))
+            dqt[k] = o
+
+        def quant_feat(k):
+            c = keep.tile([P, 512], U32, name=f"featc{k}", align_bytes=64)
+            s = keep.tile([P, 512], U8, name=f"feats{k}", align_bytes=64)
+            nc.vector.quantize_mx(
+                out=c[:].bitcast(E5M2), scales=s[:], in_=dqt[k][:].rearrange("p j n t -> p (j n t)")
+            )
+            featc[k] = c
+            feats[k] = s
+
+        inter = {}
+        chc = {}
+        chs = {}
+
+        def fill_copy(ch, eng):
+            kind, i, h = ch
+            o = work.tile([P, 512, 4], BF16, name="il_t", align_bytes=64)
+            dst = o[:].rearrange("p (c i) t -> p c t i", i=4)
+            src = raw[kind, i][:, :, 512 * h : 512 * h + 512].rearrange("p t (c i) -> p c t i", i=4)
+            if eng == "s":
+                nc.scalar.copy(out=dst, in_=src)
+            else:
+                nc.vector.tensor_copy(out=dst, in_=src)
+            inter[ch] = o
+
+        def fill_quant(ch):
+            kind, i, h = ch
+            c = keep.tile([P, 512], U32, name=f"c{kind}{i}{h}", align_bytes=64)
+            s = keep.tile([P, 512], U8, name=f"s{kind}{i}{h}", align_bytes=64)
+            nc.vector.quantize_mx(
+                out=c[:].bitcast(E4M3), scales=s[:], in_=inter[ch][:].rearrange("p n t -> p (n t)")
+            )
+            chc[ch] = c
+            chs[ch] = s
+
+        def out_rows(lhs, rhs_kind, dst, engines):
+            st = pst.tile([P, 1024], F32, name="st_t")
+            for h in range(2):
+                acc = pacc.tile([P, 512], F32, name="acc_t")
+                for n, (c, s, cols) in enumerate(lhs):
+                    nc.tensor.matmul_mx(
+                        out=acc[:],
+                        lhsT=c[:, cols].bitcast(E5M2),
+                        lhsT_scale=s[:, cols],
+                        rhs=chc[rhs_kind, n, h][:].bitcast(E4M3),
+                        rhs_scale=chs[rhs_kind, n, h][:],
+                        start=(n == 0),
+                        stop=(n == len(lhs) - 1),
+                    )
+                if engines[h] == "s":
+                    nc.scalar.copy(out=st[:, 512 * h : 512 * h + 512], in_=acc[:])
+                else:
+                    nc.vector.tensor_copy(out=st[:, 512 * h : 512 * h + 512], in_=acc[:])
+            nc.sync.dma_start(out=dst, in_=st[:])
+
+        def out0(g, engines):
+            dst = out_0[0, 512 * g : 512 * g + 512, :].rearrange("(p j) d -> j p d", j=4)
+            for j in range(4):
+                cols = slice(P * j, P * j + P)
+                lhs = [(featc[3 * g + n], feats[3 * g + n], cols) for n in range(3)]
+                out_rows(lhs, "w", dst[j], engines)
+
+        def out1(grp, engines):
+            dst = out_1[512 * grp : 512 * grp + 512, :].rearrange("(p t) d -> t p d", t=4)
+            for t in range(4):
+                cols = slice(P * t, P * t + P)
+                lhs = [(tokc[3 * g + grp], toks[3 * g + grp], cols) for g in range(2)]
+                out_rows(lhs, "x", dst[t], engines)
+
+        s_fill = {
+            0: [("w", 0, 0), ("w", 0, 1)],
+            1: [("w", 1, 0), ("w", 1, 1)],
+            2: [("w", 2, 0), ("w", 2, 1)],
+            3: [("x", 1, 0)],
+        }
+        v_fill = {1: [("x", 0, 0)], 2: [("x", 0, 1)], 3: [("x", 1, 1)]}
+
+        step_abs(0)
+        step_abs(1)
+        trig(0)
+        for k in range(6):
+            ua, ub = 2 * k, 2 * k + 1
+            units = [ua, ub]
+            ropes = [u for u in units if u % 6 != 5]
+            if k == 0:
+                load_w(2)
+                load_x(0)
+                load_unit(6)
+                load_unit(7)
+                load_x(1)
+                for u in range(8, 12):
+                    load_unit(u)
+            if k < 5:
+                step_abs(2 * k + 2)
+                step_abs(2 * k + 3)
+            if k == 0:
+                trig(1)
+            new_dq(k)
+            for u in units:
+                step_cmp(u)
+            for u in units:
+                step_mask(u)
+            for ch in s_fill.get(k, []):
+                fill_copy(ch, "s")
+            for u in ropes:
+                step_cos(u)
+            if k > 0:
+                quant_feat(k - 1)
+            for u in ropes:
+                step_sin(u)
+            if k == 3:
+                out0(0, "ss")
+            if k == 4:
+                out1(0, "ss")
+            if k == 5:
+                out1(1, "ss")
+            for ch in v_fill.get(k, []):
+                fill_copy(ch, "v")
+            for u in ropes:
+                step_add(u)
+            for ch in s_fill.get(k, []) + v_fill.get(k, []):
+                fill_quant(ch)
+            quant_tok(k)
+            transposes(k)
+        out1(2, "sv")
+        quant_feat(5)
+        out0(1, "sv")

@@ -21,6 +21,21 @@ ALU = mybir.AluOpType
 ACT = mybir.ActivationFunctionType
 
 P = 128
+SEQ = (2, 0, 1, 3, 5, 4)
+SEQ_G = (0, 2, 1)
+LOADS = (5, 4, 0, "w2", 1, 2, 3, "w0", "w1", 6, 7, "x0", "x1", 11, 10, 8, 9)
+FILLS = {
+    0: (("w20", "s"),),
+    1: (("w00", "s"), ("w01", "s"), ("w21", "g")),
+    2: (("w11", "s"), ("x00", "s"), ("w10", "g")),
+    3: (("x10", "s"), ("x01", "g"), ("x11", "v")),
+}
+LATE = ("w20", "w01", "x00")
+EV = {1: "ssssssss", 2: "ssssssss", 3: "ssssssss", 4: "ssssssss", 5: "ssssssss", 6: "ssss"}
+QF_EARLY = (3,)
+ABS_AFTER = ()
+EV_TAIL = "svsvsvsvsvsvsvsvsvsvsvsvsv"
+NOPEN = 2
 
 
 def tile_dbrxattention_pa_v_kernel(
@@ -30,13 +45,15 @@ def tile_dbrxattention_pa_v_kernel(
     with ExitStack() as ctx:
         const = ctx.enter_context(tc.tile_pool(name="const", bufs=1))
         keep = ctx.enter_context(tc.tile_pool(name="keep", bufs=1))
-        pq = ctx.enter_context(tc.tile_pool(name="pq", bufs=6))
-        pg = ctx.enter_context(tc.tile_pool(name="pg", bufs=8))
-        praw = ctx.enter_context(tc.tile_pool(name="praw", bufs=3))
-        work = ctx.enter_context(tc.tile_pool(name="work", bufs=3))
-        pst = ctx.enter_context(tc.tile_pool(name="pst", bufs=4))
-        ptp = ctx.enter_context(tc.psum_pool(name="ptp", bufs=3))
-        pacc = ctx.enter_context(tc.psum_pool(name="pacc", bufs=5))
+        pq = ctx.enter_context(tc.tile_pool(name="pq", bufs=3))
+        pg = ctx.enter_context(tc.tile_pool(name="pg", bufs=4))
+        praw = ctx.enter_context(tc.tile_pool(name="praw", bufs=4))
+        pil = ctx.enter_context(tc.tile_pool(name="pil", bufs=4))
+        work1 = ctx.enter_context(tc.tile_pool(name="work1", bufs=1))
+        work2 = ctx.enter_context(tc.tile_pool(name="work2", bufs=2))
+        pst = ctx.enter_context(tc.tile_pool(name="pst", bufs=5))
+        ptp = ctx.enter_context(tc.psum_pool(name="ptp", bufs=2))
+        pacc = ctx.enter_context(tc.psum_pool(name="pacc", bufs=6))
         ctx.enter_context(tc.manual_schedule())
 
         qt = {}
@@ -55,12 +72,15 @@ def tile_dbrxattention_pa_v_kernel(
             else:
                 sv = v_pre[0, :, rows, :]
                 gr = grad_2[0, :, rows, :]
-            q_t = pq.tile([P, 2, 512], F32, name="q_t")
-            nc.sync.dma_start(out=q_t[:], in_=sv.rearrange("h (p j) c -> p h (j c)", j=4))
-            g_t = pg.tile([P, 2, 512], BF16, name="g_t")
-            nc.sync.dma_start(out=g_t[:], in_=gr.rearrange("h (p j) c -> p h (j c)", j=4))
-            qt[u] = q_t
-            gt[u] = g_t
+            k, s = divmod(u, 2)
+            if k not in qt:
+                q_t = pq.tile([P, 4, 512], F32, name="q_t")
+                g_t = pg.tile([P, 4, 512], BF16, name="g_t")
+                qt[k] = q_t
+                gt[k] = g_t
+            hs = slice(2 * s, 2 * s + 2)
+            nc.sync.dma_start(out=qt[k][:, hs, :], in_=sv.rearrange("h (p j) c -> p h (j c)", j=4))
+            nc.sync.dma_start(out=gt[k][:, hs, :], in_=gr.rearrange("h (p j) c -> p h (j c)", j=4))
 
         def load_w(i):
             r = praw.tile([P, 4, 1024], BF16, name="raw_t")
@@ -76,72 +96,107 @@ def tile_dbrxattention_pa_v_kernel(
             )
             raw["x", i] = r
 
-        tok = const.tile([P, 8], F32, name="tok")
+        def do_load(ld):
+            if isinstance(ld, int):
+                load_unit(ld)
+            elif ld[0] == "w":
+                load_w(int(ld[1]))
+            else:
+                load_x(int(ld[1]))
+
+        for ld in LOADS[:4]:
+            do_load(ld)
+
+        ones = const.tile([P, 1], F32, name="ones")
+        nc.vector.memset(ones[:], 1.0)
+        sgn = const.tile([P, 2], F32, name="sgn")
+        nc.vector.memset(sgn[:, 0:1], 1.0)
+        nc.vector.memset(sgn[:, 1:2], -1.0)
+        ident_f = const.tile([P, P], F32, name="ident_f")
+        make_identity(nc, ident_f[:])
+        tok = const.tile([P, 512], F32, name="tok")
         nc.gpsimd.iota(
-            tok[:].rearrange("p (g j) -> p g j", j=4),
-            [[512, 2], [1, 4]],
+            tok[:].rearrange("p (j n) -> p j n", j=4),
+            [[1, 4], [4, 128]],
             base=0,
-            channel_multiplier=4,
+            channel_multiplier=0,
             allow_small_or_imprecise_dtypes=True,
         )
         ident = const.tile([P, P], BF16, name="ident")
         make_identity(nc, ident[:])
-        sgn = const.tile([P, 2], F32, name="sgn")
-        nc.vector.memset(sgn[:, 0:1], 1.0)
-        nc.vector.memset(sgn[:, 1:2], -1.0)
         warm = const.tile([P, 1], F32, name="warm")
-        nc.scalar.activation(warm[:], sgn[:, 0:1], ACT.Sin)
+        nc.scalar.activation(warm[:], ones[:], ACT.Sin)
 
-        load_unit(0)
-        load_unit(1)
-        load_w(0)
-        load_unit(2)
-        load_unit(3)
-        load_w(1)
-        load_unit(4)
-        load_unit(5)
-
-        y = const.tile([P, 8, 64], F32, name="y")
-        for i in range(64):
-            c = ROPE_BASE ** (-2.0 * i / HD) / (2.0 * math.pi)
-            if i % 5 < 3:
-                nc.vector.tensor_scalar_mul(y[:, :, i], tok[:], c)
-            else:
-                nc.scalar.activation(y[:, :, i], tok[:], ACT.Copy, scale=c)
-        n_i = const.tile([P, 8, 64], I32, name="n_i")
-        nc.vector.tensor_copy(out=n_i[:], in_=y[:])
-        f = const.tile([P, 8, 64], F32, name="f")
-        nc.vector.tensor_tensor(out=f[:], in0=y[:], in1=n_i[:], op=ALU.subtract)
-        fa = const.tile([P, 8, 64], F32, name="fa")
-        nc.scalar.activation(fa[:], f[:], ACT.Abs)
-        f2 = const.tile([P, 8, 64, 2], F32, name="f2")
+        ca = const.tile([P, 8], F32, name="ca")
+        cb = const.tile([P, 8], F32, name="cb")
+        for i in range(8):
+            nc.vector.tensor_scalar_mul(cb[:, i : i + 1], ones[:], ROPE_BASE ** (-2.0 * i / HD))
+            nc.scalar.activation(
+                ca[:, i : i + 1], ones[:], ACT.Copy, scale=ROPE_BASE ** (-16.0 * i / HD) / (2.0 * math.pi)
+            )
+        cbs = const.tile([P, 8, 2], F32, name="cbs")
         nc.vector.tensor_tensor(
-            out=f2[:],
-            in0=f[:].unsqueeze(3).to_broadcast([P, 8, 64, 2]),
-            in1=sgn[:].unsqueeze(1).unsqueeze(1).to_broadcast([P, 8, 64, 2]),
+            out=cbs[:],
+            in0=cb[:].unsqueeze(2).to_broadcast([P, 8, 2]),
+            in1=sgn[:].unsqueeze(1).to_broadcast([P, 8, 2]),
             op=ALU.mult,
         )
-        fc = const.tile([P, 8, 64], F32, name="fc")
-        nc.vector.tensor_scalar(
-            out=fc[:], in0=fa[:], scalar1=-1.0, scalar2=0.25, op0=ALU.mult, op1=ALU.add
+        row = const.tile([P, 8, 16], F32, name="row")
+        nc.vector.tensor_tensor(
+            out=row[:],
+            in0=ca[:].unsqueeze(2).to_broadcast([P, 8, 16]),
+            in1=cbs[:].rearrange("p b e -> p (b e)").unsqueeze(1).to_broadcast([P, 8, 16]),
+            op=ALU.mult,
         )
-        cos_t = []
-        sin_t = []
-        for g in range(2):
-            cg = const.tile([P, 4, 64, 2], F32, name=f"cos{g}")
-            cos_t.append(cg)
-            sg = const.tile([P, 4, 64, 2], F32, name=f"sin{g}")
-            sin_t.append(sg)
+        col_p = ptp.tile([P, P], F32, name="tp_t")
+        nc.tensor.transpose(col_p[:], row[:].rearrange("p a b -> p (a b)"), ident_f[:])
+        col = const.tile([P, 1], F32, name="col")
+        nc.vector.tensor_copy(out=col[:], in_=col_p[:, 0:1])
+
+        cos_p = {}
+        sin_p = {}
+        sin_s = {}
+        fr = {}
+
+        def turns(g):
+            y = const.tile([P, 512], F32, name="y_t")
+            nc.vector.tensor_scalar(
+                out=y[:], in0=tok[:], scalar1=512.0 * g, scalar2=col[:], op0=ALU.add, op1=ALU.mult
+            )
+            n_i = const.tile([P, 512], I32, name="n_t")
+            nc.vector.tensor_copy(out=n_i[:], in_=y[:])
+            f = const.tile([P, 512], F32, name="f_t")
+            nc.vector.tensor_tensor(out=f[:], in0=y[:], in1=n_i[:], op=ALU.subtract)
+            fr[g] = f
 
         def trig(g):
-            js = slice(4 * g, 4 * g + 4)
-            nc.scalar.activation(
-                cos_t[g][:],
-                fc[:, js, :].unsqueeze(3).to_broadcast([P, 4, 64, 2]),
-                ACT.Sin,
-                scale=2.0 * math.pi,
+            f = fr[g]
+            fa = const.tile([P, 512], F32, name="fa_t")
+            nc.scalar.activation(fa[:], f[:], ACT.Abs)
+            sv = const.tile([P, 512], F32, name=f"sv{g}")
+            nc.scalar.activation(sv[:], f[:], ACT.Sin, scale=2.0 * math.pi)
+            fc = const.tile([P, 512], F32, name="fc_t")
+            nc.vector.tensor_scalar(
+                out=fc[:], in0=fa[:], scalar1=-1.0, scalar2=0.25, op0=ALU.mult, op1=ALU.add
             )
-            nc.scalar.activation(sin_t[g][:], f2[:, js, :, :], ACT.Sin, scale=2.0 * math.pi)
+            cv = const.tile([P, 512], F32, name=f"cv{g}")
+            nc.scalar.activation(cv[:], fc[:], ACT.Sin, scale=2.0 * math.pi)
+            return sv, cv
+
+        def tables_p(g, sv, cv):
+            cp = pacc.tile([P, 4, P], F32, name="acc_t")
+            for j in range(4):
+                nc.tensor.transpose(cp[:, j, :], cv[:, P * j : P * j + P], ident_f[:])
+            sp = pacc.tile([P, 4, P], F32, name="acc_t")
+            for j in range(4):
+                nc.tensor.transpose(sp[:, j, :], sv[:, P * j : P * j + P], ident_f[:])
+            cos_p[g] = cp
+            sin_p[g] = sp
+
+        def tables_s(g):
+            ss = const.tile([P, 4, P], F32, name=f"sin_s{g}")
+            nc.scalar.copy(out=ss[:], in_=sin_p[g][:])
+            sin_s[g] = ss
 
         ha = {}
         mk = {}
@@ -151,73 +206,84 @@ def tile_dbrxattention_pa_v_kernel(
         dq = {}
 
         def step_abs(u):
-            a = work.tile([P, 1024], BF16, name="ha_t")
+            k, s = divmod(u, 2)
+            if k not in ha:
+                a = work2.tile([P, 4, 512], BF16, name="ha_t")
+                ha[k] = a
+            hs = slice(2 * s, 2 * s + 2)
             top = (
-                qt[u][:]
+                qt[k][:, hs, :]
                 .rearrange("p h n -> p (h n)")
                 .bitcast(BF16)
                 .rearrange("p (n e) -> p n e", e=2)[:, :, 1]
             )
-            nc.scalar.activation(a[:], top, ACT.Abs)
-            ha[u] = a
+            nc.scalar.activation(ha[k][:, hs, :].rearrange("p h n -> p (h n)"), top, ACT.Abs)
 
-        def step_cmp(u):
-            m = work.tile([P, 1024], BF16, name="mk_t")
-            nc.vector.tensor_scalar(
-                out=m[:], in0=ha[u][:], scalar1=CLAMP, scalar2=None, op0=ALU.is_lt
-            )
-            mk[u] = m
-
-        def new_dq(k):
-            d_t = work.tile([P, 4, P, 4], BF16, name="dq_t", align_bytes=64)
+        def new_group(k):
+            m = work1.tile([P, 4, 512], BF16, name="mk_t")
+            mk[k] = m
+            d_t = work2.tile([P, 512, 4], BF16, name="dq_t", align_bytes=64)
             dq[k] = d_t
+            nh = 2 if k % 3 == 2 else 4
+            g_m = work1.tile([P, nh, 4, 64, 2], BF16, name="gm_t")
+            gm[k] = g_m
+            a = work1.tile([P, 4, nh, P], F32, name="t1_t")
+            t1[k] = a
+            b = work1.tile([P, 4, nh, P], F32, name="t2_t")
+            t2[k] = b
 
-        def step_mask(u):
-            k, s = divmod(u, 2)
-            if u % 6 == 5:
-                for h in range(2):
-                    nc.vector.tensor_tensor(
-                        out=dq[k][:, :, 64 + 32 * h : 96 + 32 * h, :].rearrange("p t q j -> p q j t"),
-                        in0=mk[u][:, 512 * h : 512 * h + 512].rearrange("p (j q t) -> p q j t", j=4, t=4),
-                        in1=gt[u][:, h, :].rearrange("p (j q t) -> p q j t", j=4, t=4),
-                        op=ALU.mult,
-                    )
-            else:
-                g_m = work.tile([P, 2, 4, 64, 2], BF16, name="gm_t")
+        def step_cmp(k, h0, h1):
+            nc.vector.tensor_scalar(
+                out=mk[k][:, h0:h1, :].rearrange("p h n -> p (h n)"),
+                in0=ha[k][:, h0:h1, :].rearrange("p h n -> p (h n)"),
+                scalar1=CLAMP,
+                scalar2=None,
+                op0=ALU.is_lt,
+            )
+
+        def step_mask_v(k):
+            for h in range(2, 4):
                 nc.vector.tensor_tensor(
-                    out=g_m[:].rearrange("p h j i e -> p (h j i e)"),
-                    in0=mk[u][:],
-                    in1=gt[u][:].rearrange("p h n -> p (h n)"),
+                    out=dq[k][:, P * h : P * h + P, :].rearrange("p (q t) j -> p q j t", t=4),
+                    in0=mk[k][:, h, :].rearrange("p (j q t) -> p q j t", j=4, t=4),
+                    in1=gt[k][:, h, :].rearrange("p (j q t) -> p q j t", j=4, t=4),
                     op=ALU.mult,
                 )
-                gm[u] = g_m
 
-        def step_cos(u):
-            a = work.tile([P, 4, 2, P], F32, name="t1_t")
+        def step_mask(k, h0, h1):
             nc.vector.tensor_tensor(
-                out=a[:].rearrange("p j h c -> p h j c"),
-                in0=gm[u][:].rearrange("p h j i e -> p h j (i e)"),
-                in1=cos_t[u // 6][:].rearrange("p j i e -> p j (i e)").unsqueeze(1).to_broadcast([P, 2, 4, P]),
+                out=gm[k][:, h0:h1].rearrange("p h j i e -> p (h j i e)"),
+                in0=mk[k][:, h0:h1, :].rearrange("p h n -> p (h n)"),
+                in1=gt[k][:, h0:h1, :].rearrange("p h n -> p (h n)"),
                 op=ALU.mult,
             )
-            t1[u] = a
 
-        def step_sin(u):
-            a = work.tile([P, 4, 2, P], F32, name="t2_t")
+        def step_cos(k, h0, h1):
             nc.vector.tensor_tensor(
-                out=a[:].rearrange("p j h (i e) -> p h j i e", e=2),
-                in0=gm[u][:, :, :, :, ::-1],
-                in1=sin_t[u // 6][:].unsqueeze(1).to_broadcast([P, 2, 4, 64, 2]),
+                out=t1[k][:, :, h0:h1, :].rearrange("p j h c -> p h j c"),
+                in0=gm[k][:, h0:h1].rearrange("p h j i e -> p h j (i e)"),
+                in1=cos_p[k // 3][:].unsqueeze(1).to_broadcast([P, h1 - h0, 4, P]),
                 op=ALU.mult,
             )
-            t2[u] = a
 
-        def step_add(u):
-            k, s = divmod(u, 2)
+        def step_sin(k, h0, h1, eng):
+            tab = sin_p[k // 3] if eng == "v" else sin_s[k // 3]
+            e = nc.vector if eng == "v" else nc.gpsimd
+            e.tensor_tensor(
+                out=t2[k][:, :, h0:h1, :].rearrange("p j h (i e) -> p h j i e", e=2),
+                in0=gm[k][:, h0:h1, :, :, ::-1],
+                in1=tab[:]
+                .rearrange("p j (i e) -> p j i e", e=2)
+                .unsqueeze(1)
+                .to_broadcast([P, h1 - h0, 4, 64, 2]),
+                op=ALU.mult,
+            )
+
+        def step_add(k, h0, h1):
             nc.vector.tensor_tensor(
-                out=dq[k][:, :, 64 * s : 64 * s + 64, :].rearrange("p t q j -> p q j t"),
-                in0=t1[u][:].rearrange("p j h (q t) -> p (h q) j t", t=4),
-                in1=t2[u][:].rearrange("p j h (q t) -> p (h q) j t", t=4),
+                out=dq[k][:, P * h0 : P * h1, :].rearrange("p (q t) j -> p q j t", t=4),
+                in0=t1[k][:, :, h0:h1, :].rearrange("p j h (q t) -> p (h q) j t", t=4),
+                in1=t2[k][:, :, h0:h1, :].rearrange("p j h (q t) -> p (h q) j t", t=4),
                 op=ALU.add,
             )
 
@@ -226,34 +292,43 @@ def tile_dbrxattention_pa_v_kernel(
         featc = {}
         feats = {}
 
-        def quant_tok(k):
-            c = keep.tile([P, 512], U32, name=f"tokc{k}", align_bytes=64)
-            s = keep.tile([P, 512], U8, name=f"toks{k}", align_bytes=64)
+        def quant_tok(u):
+            k, half = divmod(u, 2)
+            c = keep.tile([P, 256], U32, name=f"tokc{u}", align_bytes=64)
+            s = keep.tile([P, 256], U8, name=f"toks{u}", align_bytes=64)
             nc.vector.quantize_mx(
-                out=c[:].bitcast(E5M2), scales=s[:], in_=dq[k][:].rearrange("p t q j -> p (t q j)")
+                out=c[:].bitcast(E5M2),
+                scales=s[:],
+                in_=dq[k][:, 256 * half : 256 * half + 256, :].rearrange("p c j -> p (c j)"),
             )
-            tokc[k] = c
-            toks[k] = s
+            tokc[u] = c
+            toks[u] = s
 
         dqt = {}
 
-        def transposes(k):
-            o = work.tile([P, 4, P, 4], BF16, name="dqt_t", align_bytes=64)
-            for j in range(4):
+        def transposes(k, half, engines):
+            o = work2.tile([P, 2, P, 4], BF16, name=f"dqt{half}", align_bytes=64)
+            for jj in range(2):
+                j = 2 * half + jj
                 tp = ptp.tile([P, 4, P], BF16, name="tp_t")
                 for t in range(4):
-                    nc.tensor.transpose(tp[:, t, :], dq[k][:, t, :, j], ident[:])
-                nc.scalar.copy(out=o[:, j], in_=tp[:].rearrange("p t n -> p n t"))
-            dqt[k] = o
+                    nc.tensor.transpose(tp[:, t, :], dq[k][:, t::4, j], ident[:])
+                if engines[jj] == "s":
+                    nc.scalar.copy(out=o[:, jj], in_=tp[:].rearrange("p t n -> p n t"))
+                else:
+                    nc.vector.tensor_copy(out=o[:, jj], in_=tp[:].rearrange("p t n -> p n t"))
+            dqt[k, half] = o
 
-        def quant_feat(k):
-            c = keep.tile([P, 512], U32, name=f"featc{k}", align_bytes=64)
-            s = keep.tile([P, 512], U8, name=f"feats{k}", align_bytes=64)
+        def quant_feat(k, half):
+            c = keep.tile([P, 256], U32, name=f"featc{k}{half}", align_bytes=64)
+            s = keep.tile([P, 256], U8, name=f"feats{k}{half}", align_bytes=64)
             nc.vector.quantize_mx(
-                out=c[:].bitcast(E5M2), scales=s[:], in_=dqt[k][:].rearrange("p j n t -> p (j n t)")
+                out=c[:].bitcast(E5M2),
+                scales=s[:],
+                in_=dqt[k, half][:].rearrange("p j n t -> p (j n t)"),
             )
-            featc[k] = c
-            feats[k] = s
+            featc[k, half] = c
+            feats[k, half] = s
 
         inter = {}
         chc = {}
@@ -261,10 +336,19 @@ def tile_dbrxattention_pa_v_kernel(
 
         def fill_copy(ch, eng):
             kind, i, h = ch
-            o = work.tile([P, 512, 4], BF16, name="il_t", align_bytes=64)
+            o = pil.tile([P, 512, 4], BF16, name="il_t", align_bytes=64)
             dst = o[:].rearrange("p (c i) t -> p c t i", i=4)
             src = raw[kind, i][:, :, 512 * h : 512 * h + 512].rearrange("p t (c i) -> p c t i", i=4)
-            if eng == "s":
+            if eng == "g":
+                nc.gpsimd.tensor_scalar(
+                    out=o[:],
+                    in0=raw[kind, i][:, :, 512 * h : 512 * h + 512].rearrange("p t c -> p c t"),
+                    scalar1=1.0,
+                    scalar2=0.0,
+                    op0=ALU.mult,
+                    op1=ALU.add,
+                )
+            elif eng == "s":
                 nc.scalar.copy(out=dst, in_=src)
             else:
                 nc.vector.tensor_copy(out=dst, in_=src)
@@ -280,95 +364,190 @@ def tile_dbrxattention_pa_v_kernel(
             chc[ch] = c
             chs[ch] = s
 
-        def out_rows(lhs, rhs_kind, dst, engines):
+        def passes(acc, lhs, kind, h, lo, hi):
+            for n in range(lo, hi):
+                c, s, cols = lhs[n]
+                nc.tensor.matmul_mx(
+                    out=acc[:],
+                    lhsT=c[:, cols].bitcast(E5M2),
+                    lhsT_scale=s[:, cols],
+                    rhs=chc[kind, SEQ_G[n] if kind == "w" else n, h][:].bitcast(E4M3),
+                    rhs_scale=chs[kind, SEQ_G[n] if kind == "w" else n, h][:],
+                    start=(n == 0),
+                    stop=(n == len(lhs) - 1),
+                )
+
+        def evac(st, acc, h, eng):
+            if eng == "s":
+                nc.scalar.copy(out=st[:, 512 * h : 512 * h + 512], in_=acc[:])
+            else:
+                nc.vector.tensor_copy(out=st[:, 512 * h : 512 * h + 512], in_=acc[:])
+
+        def lhs0(g, j, n):
+            kk = 3 * g + SEQ_G[n]
+            return featc[kk, j // 2], feats[kk, j // 2], slice(P * (j % 2), P * (j % 2) + P)
+
+        def out0_row(g, j, engines):
+            dst = out_0[0, 512 * g : 512 * g + 512, :].rearrange("(p j) d -> j p d", j=4)[j]
             st = pst.tile([P, 1024], F32, name="st_t")
+            lhs = [lhs0(g, j, n) for n in range(3)]
             for h in range(2):
                 acc = pacc.tile([P, 512], F32, name="acc_t")
-                for n, (c, s, cols) in enumerate(lhs):
-                    nc.tensor.matmul_mx(
-                        out=acc[:],
-                        lhsT=c[:, cols].bitcast(E5M2),
-                        lhsT_scale=s[:, cols],
-                        rhs=chc[rhs_kind, n, h][:].bitcast(E4M3),
-                        rhs_scale=chs[rhs_kind, n, h][:],
-                        start=(n == 0),
-                        stop=(n == len(lhs) - 1),
-                    )
-                if engines[h] == "s":
-                    nc.scalar.copy(out=st[:, 512 * h : 512 * h + 512], in_=acc[:])
-                else:
-                    nc.vector.tensor_copy(out=st[:, 512 * h : 512 * h + 512], in_=acc[:])
+                passes(acc, lhs, "w", h, 0, 3)
+                evac(st, acc, h, engines[h])
             nc.sync.dma_start(out=dst, in_=st[:])
 
-        def out0(g, engines):
-            dst = out_0[0, 512 * g : 512 * g + 512, :].rearrange("(p j) d -> j p d", j=4)
-            for j in range(4):
-                cols = slice(P * j, P * j + P)
-                lhs = [(featc[3 * g + n], feats[3 * g + n], cols) for n in range(3)]
-                out_rows(lhs, "w", dst[j], engines)
+        early = {}
 
-        def out1(grp, engines):
-            dst = out_1[512 * grp : 512 * grp + 512, :].rearrange("(p t) d -> t p d", t=4)
-            for t in range(4):
-                cols = slice(P * t, P * t + P)
-                lhs = [(tokc[3 * g + grp], toks[3 * g + grp], cols) for g in range(2)]
-                out_rows(lhs, "x", dst[t], engines)
+        def out0_open(g, j):
+            lhs = [lhs0(g, j, n) for n in range(2)] + [None]
+            for h in range(2):
+                acc = pacc.tile([P, 512], F32, name="acc_t")
+                passes(acc, lhs, "w", h, 0, 2)
+                early[g, j, h] = acc
 
-        s_fill = {
-            0: [("w", 0, 0), ("w", 0, 1)],
-            1: [("w", 1, 0), ("w", 1, 1)],
-            2: [("w", 2, 0), ("w", 2, 1)],
-            3: [("x", 1, 0)],
-        }
-        v_fill = {1: [("x", 0, 0)], 2: [("x", 0, 1)], 3: [("x", 1, 1)]}
+        def out0_close(g, j, engines):
+            dst = out_0[0, 512 * g : 512 * g + 512, :].rearrange("(p j) d -> j p d", j=4)[j]
+            st = pst.tile([P, 1024], F32, name="st_t")
+            lhs = [None, None, lhs0(g, j, 2)]
+            for h in range(2):
+                passes(early[g, j, h], lhs, "w", h, 2, 3)
+                evac(st, early[g, j, h], h, engines[h])
+            nc.sync.dma_start(out=dst, in_=st[:])
 
-        step_abs(0)
-        step_abs(1)
-        trig(0)
-        for k in range(6):
-            ua, ub = 2 * k, 2 * k + 1
-            units = [ua, ub]
-            ropes = [u for u in units if u % 6 != 5]
-            if k == 0:
-                load_w(2)
-                load_x(0)
-                load_unit(6)
-                load_unit(7)
-                load_x(1)
-                for u in range(8, 12):
-                    load_unit(u)
-            if k < 5:
-                step_abs(2 * k + 2)
-                step_abs(2 * k + 3)
-            if k == 0:
-                trig(1)
-            new_dq(k)
-            for u in units:
-                step_cmp(u)
-            for u in units:
-                step_mask(u)
-            for ch in s_fill.get(k, []):
-                fill_copy(ch, "s")
-            for u in ropes:
-                step_cos(u)
-            if k > 0:
-                quant_feat(k - 1)
-            for u in ropes:
-                step_sin(u)
-            if k == 3:
-                out0(0, "ss")
-            if k == 4:
-                out1(0, "ss")
-            if k == 5:
-                out1(1, "ss")
-            for ch in v_fill.get(k, []):
-                fill_copy(ch, "v")
-            for u in ropes:
-                step_add(u)
-            for ch in s_fill.get(k, []) + v_fill.get(k, []):
-                fill_quant(ch)
-            quant_tok(k)
-            transposes(k)
-        out1(2, "sv")
-        quant_feat(5)
-        out0(1, "sv")
+        def out1_row(pr, h, engines):
+            rows = slice(256 * pr + P * h, 256 * pr + P * h + P)
+            st = pst.tile([P, 1024], F32, name="st_t")
+            cols = slice(P * h, P * h + P)
+            lhs = [(tokc[6 * g + pr], toks[6 * g + pr], cols) for g in range(2)]
+            for hh in range(2):
+                acc = pacc.tile([P, 512], F32, name="acc_t")
+                passes(acc, lhs, "x", hh, 0, 2)
+                evac(st, acc, hh, engines[hh])
+            nc.sync.dma_start(out=out_1[rows, :], in_=st[:])
+
+        def ch_of(c):
+            return c[0], int(c[1]), int(c[2])
+
+        g_first = SEQ[0] // 3
+        k0 = SEQ[0]
+        new_group(k0)
+        turns(g_first)
+        step_abs(2 * k0 + 1)
+        step_cmp(k0, 2, 4)
+        tabs = {}
+        tabs[g_first] = trig(g_first)
+        step_abs(2 * k0)
+        step_mask_v(k0)
+        tables_p(g_first, *tabs[g_first])
+        tables_s(g_first)
+        step_cmp(k0, 0, 2)
+        turns(1 - g_first)
+        for ld in LOADS[4:]:
+            do_load(ld)
+        for n in range(6):
+            k = SEQ[n]
+            v_unit = k % 3 == 2
+            last = n == 5
+            fills = FILLS.get(n, ())
+            gf = [c for c, e in fills if e == "g"]
+            if v_unit:
+                if n > 0:
+                    step_mask_v(k)
+                    quant_tok(2 * k + 1)
+                if n in QF_EARLY:
+                    quant_feat(SEQ[n - 1], 0)
+                    quant_feat(SEQ[n - 1], 1)
+                step_mask(k, 0, 2)
+                step_cos(k, 0, 2)
+                step_sin(k, 1, 2, "g")
+                step_sin(k, 0, 1, "v")
+            else:
+                step_mask(k, 0, 2)
+                if n in QF_EARLY:
+                    quant_feat(SEQ[n - 1], 0)
+                    quant_feat(SEQ[n - 1], 1)
+                step_mask(k, 2, 4)
+                step_cos(k, 0, 4)
+                if gf:
+                    step_sin(k, 3, 4, "g")
+                    fill_copy(ch_of(gf[0]), "g")
+                    step_sin(k, 0, 3, "v")
+                else:
+                    step_sin(k, 2, 4, "g")
+                    step_sin(k, 0, 2, "v")
+            if not last and n not in ABS_AFTER:
+                step_abs(2 * SEQ[n + 1])
+                step_abs(2 * SEQ[n + 1] + 1)
+            if n > 0 and n not in QF_EARLY:
+                quant_feat(SEQ[n - 1], 0)
+                quant_feat(SEQ[n - 1], 1)
+            for c, e in FILLS.get(n - 1, ()):
+                if e == "s" and c in LATE:
+                    fill_quant(ch_of(c))
+            if n == 0:
+                tabs[1 - g_first] = trig(1 - g_first)
+            for c, e in fills:
+                if e == "s":
+                    fill_copy(ch_of(c), "s")
+            if n > 0:
+                p = SEQ[n - 1]
+                if all(q in SEQ[:n] for q in (p % 3, p % 3 + 3)):
+                    for h in range(2 if p % 3 == 2 else 4):
+                        out1_row(2 * (p % 3) + h // 2, h % 2, EV[n][2 * h : 2 * h + 2])
+                if n == 4:
+                    out1_row(5, 0, "ss")
+                    out1_row(5, 1, "ss")
+                g = p // 3
+                if all(q in SEQ[:n] for q in (3 * g, 3 * g + 1, 3 * g + 2)):
+                    for j in range(4):
+                        out0_row(g, j, EV[n][2 * j : 2 * j + 2])
+            if not last and n in ABS_AFTER:
+                step_abs(2 * SEQ[n + 1])
+                step_abs(2 * SEQ[n + 1] + 1)
+            if last:
+                for j in range(NOPEN):
+                    out0_open(k // 3, j)
+                step_add(k, 0, 2)
+                step_add(k, 2, 4)
+                quant_tok(2 * k)
+            else:
+                step_add(k, 0, 2 if v_unit else 4)
+                g = SEQ[n + 1] // 3
+                if g != k // 3:
+                    tables_p(g, *tabs[g])
+                    if g not in sin_s:
+                        tables_s(g)
+                new_group(SEQ[n + 1])
+                step_cmp(SEQ[n + 1], 0, 4)
+                for c, e in fills:
+                    if e == "v":
+                        fill_copy(ch_of(c), "v")
+                for c, e in fills:
+                    if not (e == "s" and c in LATE):
+                        fill_quant(ch_of(c))
+                quant_tok(2 * k)
+                if n == 0 or not v_unit:
+                    quant_tok(2 * k + 1)
+                transposes(k, 0, "ss")
+                transposes(k, 1, "ss")
+        k = SEQ[5]
+        g = k // 3
+        transposes(k, 0, "sv")
+        quant_tok(2 * k + 1)
+        quant_feat(k, 0)
+        transposes(k, 1, "sv")
+        quant_feat(k, 1)
+        e = 0
+        for h in range(2):
+            out1_row((2 * k) % 6, h, EV_TAIL[e : e + 2])
+            e += 2
+        for j in range(NOPEN):
+            out0_close(g, j, EV_TAIL[e : e + 2])
+            e += 2
+        for h in range(2):
+            out1_row((2 * k + 1) % 6, h, EV_TAIL[e : e + 2])
+            e += 2
+        for j in range(NOPEN, 4):
+            out0_row(g, j, EV_TAIL[e : e + 2])
+            e += 2

@@ -28,14 +28,14 @@ FILLS = {
     0: (("w20", "s"),),
     1: (("w00", "s"), ("w01", "s"), ("w21", "g")),
     2: (("w11", "s"), ("x00", "s"), ("w10", "g")),
-    3: (("x10", "s"), ("x01", "g"), ("x11", "v")),
+    3: (("x10", "s"), ("x01", "g"), ("x11", "s")),
 }
-LATE = ("w20", "w01", "x00")
+LATE = ("w20", "w01", "x00", "x11")
 EV = {1: "ssssssss", 2: "ssssssss", 3: "ssssssss", 4: "ssssssss", 5: "ssssssss", 6: "ssss"}
 QF_EARLY = (3,)
 ABS_AFTER = ()
-EV_TAIL = "svsvsvsvsvsvsvsvsvsvsvsvsv"
-NOPEN = 2
+EV_TAIL = "sssvsvsvsvsvsvsvsvsvsv"
+NOPEN = 0
 
 
 def tile_dbrxattention_pa_v_kernel(
@@ -51,7 +51,7 @@ def tile_dbrxattention_pa_v_kernel(
         pil = ctx.enter_context(tc.tile_pool(name="pil", bufs=4))
         work1 = ctx.enter_context(tc.tile_pool(name="work1", bufs=1))
         work2 = ctx.enter_context(tc.tile_pool(name="work2", bufs=2))
-        pst = ctx.enter_context(tc.tile_pool(name="pst", bufs=5))
+        pst = ctx.enter_context(tc.tile_pool(name="pst", bufs=6))
         ptp = ctx.enter_context(tc.psum_pool(name="ptp", bufs=2))
         pacc = ctx.enter_context(tc.psum_pool(name="pacc", bufs=6))
         ctx.enter_context(tc.manual_schedule())
@@ -122,8 +122,6 @@ def tile_dbrxattention_pa_v_kernel(
             channel_multiplier=0,
             allow_small_or_imprecise_dtypes=True,
         )
-        ident = const.tile([P, P], BF16, name="ident")
-        make_identity(nc, ident[:])
         warm = const.tile([P, 1], F32, name="warm")
         nc.scalar.activation(warm[:], ones[:], ACT.Sin)
 
@@ -171,11 +169,11 @@ def tile_dbrxattention_pa_v_kernel(
 
         def trig(g):
             f = fr[g]
-            fa = const.tile([P, 512], F32, name="fa_t")
+            fa = const.tile([P, 512], F32, name="n_t")
             nc.scalar.activation(fa[:], f[:], ACT.Abs)
             sv = const.tile([P, 512], F32, name=f"sv{g}")
             nc.scalar.activation(sv[:], f[:], ACT.Sin, scale=2.0 * math.pi)
-            fc = const.tile([P, 512], F32, name="fc_t")
+            fc = const.tile([P, 512], F32, name="y_t")
             nc.vector.tensor_scalar(
                 out=fc[:], in0=fa[:], scalar1=-1.0, scalar2=0.25, op0=ALU.mult, op1=ALU.add
             )
@@ -222,7 +220,7 @@ def tile_dbrxattention_pa_v_kernel(
         def new_group(k):
             m = work1.tile([P, 4, 512], BF16, name="mk_t")
             mk[k] = m
-            d_t = work2.tile([P, 512, 4], BF16, name="dq_t", align_bytes=64)
+            d_t = work2.tile([P, 4, P, 4], BF16, name="dq_t", align_bytes=64)
             dq[k] = d_t
             nh = 2 if k % 3 == 2 else 4
             g_m = work1.tile([P, nh, 4, 64, 2], BF16, name="gm_t")
@@ -244,7 +242,7 @@ def tile_dbrxattention_pa_v_kernel(
         def step_mask_v(k):
             for h in range(2, 4):
                 nc.vector.tensor_tensor(
-                    out=dq[k][:, P * h : P * h + P, :].rearrange("p (q t) j -> p q j t", t=4),
+                    out=dq[k][:, :, 32 * h : 32 * h + 32, :].rearrange("p t q j -> p q j t"),
                     in0=mk[k][:, h, :].rearrange("p (j q t) -> p q j t", j=4, t=4),
                     in1=gt[k][:, h, :].rearrange("p (j q t) -> p q j t", j=4, t=4),
                     op=ALU.mult,
@@ -281,7 +279,7 @@ def tile_dbrxattention_pa_v_kernel(
 
         def step_add(k, h0, h1):
             nc.vector.tensor_tensor(
-                out=dq[k][:, P * h0 : P * h1, :].rearrange("p (q t) j -> p q j t", t=4),
+                out=dq[k][:, :, 32 * h0 : 32 * h1, :].rearrange("p t q j -> p q j t"),
                 in0=t1[k][:, :, h0:h1, :].rearrange("p j h (q t) -> p (h q) j t", t=4),
                 in1=t2[k][:, :, h0:h1, :].rearrange("p j h (q t) -> p (h q) j t", t=4),
                 op=ALU.add,
@@ -292,31 +290,38 @@ def tile_dbrxattention_pa_v_kernel(
         featc = {}
         feats = {}
 
-        def quant_tok(u):
-            k, half = divmod(u, 2)
-            c = keep.tile([P, 256], U32, name=f"tokc{u}", align_bytes=64)
-            s = keep.tile([P, 256], U8, name=f"toks{u}", align_bytes=64)
+        def quant_tok(k):
+            c = keep.tile([P, 512], U32, name=f"tokc{k}", align_bytes=64)
+            s = keep.tile([P, 512], U8, name=f"toks{k}", align_bytes=64)
             nc.vector.quantize_mx(
-                out=c[:].bitcast(E5M2),
-                scales=s[:],
-                in_=dq[k][:, 256 * half : 256 * half + 256, :].rearrange("p c j -> p (c j)"),
+                out=c[:].bitcast(E5M2), scales=s[:], in_=dq[k][:].rearrange("p t q j -> p (t q j)")
             )
-            tokc[u] = c
-            toks[u] = s
+            tokc[k] = c
+            toks[k] = s
 
         dqt = {}
 
-        def transposes(k, half, engines):
+        def transposes(k, half, eng):
             o = work2.tile([P, 2, P, 4], BF16, name=f"dqt{half}", align_bytes=64)
-            for jj in range(2):
-                j = 2 * half + jj
-                tp = ptp.tile([P, 4, P], BF16, name="tp_t")
-                for t in range(4):
-                    nc.tensor.transpose(tp[:, t, :], dq[k][:, t::4, j], ident[:])
-                if engines[jj] == "s":
-                    nc.scalar.copy(out=o[:, jj], in_=tp[:].rearrange("p t n -> p n t"))
-                else:
-                    nc.vector.tensor_copy(out=o[:, jj], in_=tp[:].rearrange("p t n -> p n t"))
+            pairs = (
+                dq[k][:]
+                .rearrange("p t q j -> p (t q j)")
+                .bitcast(F32)
+                .rearrange("p (t q w) -> p t q w", t=4, w=2)
+            )
+            tp = ptp.tile([P, 4, P], F32, name="tp_t")
+            for t in range(4):
+                nc.tensor.transpose(tp[:, t, :], pairs[:, t, :, half], ident_f[:])
+            src = (
+                tp[:]
+                .rearrange("p t n -> p (t n)")
+                .bitcast(BF16)
+                .rearrange("p (t n e) -> p e n t", t=4, e=2)
+            )
+            if eng == "s":
+                nc.scalar.copy(out=o[:], in_=src)
+            else:
+                nc.vector.tensor_copy(out=o[:], in_=src)
             dqt[k, half] = o
 
         def quant_feat(k, half):
@@ -415,16 +420,16 @@ def tile_dbrxattention_pa_v_kernel(
                 evac(st, early[g, j, h], h, engines[h])
             nc.sync.dma_start(out=dst, in_=st[:])
 
-        def out1_row(pr, h, engines):
-            rows = slice(256 * pr + P * h, 256 * pr + P * h + P)
+        def out1_row(grp, t, engines):
+            dst = out_1[512 * grp : 512 * grp + 512, :].rearrange("(p t) d -> t p d", t=4)[t]
             st = pst.tile([P, 1024], F32, name="st_t")
-            cols = slice(P * h, P * h + P)
-            lhs = [(tokc[6 * g + pr], toks[6 * g + pr], cols) for g in range(2)]
+            cols = slice(P * t, P * t + P)
+            lhs = [(tokc[3 * g + grp], toks[3 * g + grp], cols) for g in range(2)]
             for hh in range(2):
                 acc = pacc.tile([P, 512], F32, name="acc_t")
                 passes(acc, lhs, "x", hh, 0, 2)
                 evac(st, acc, hh, engines[hh])
-            nc.sync.dma_start(out=out_1[rows, :], in_=st[:])
+            nc.sync.dma_start(out=dst, in_=st[:])
 
         def ch_of(c):
             return c[0], int(c[1]), int(c[2])
@@ -454,7 +459,6 @@ def tile_dbrxattention_pa_v_kernel(
             if v_unit:
                 if n > 0:
                     step_mask_v(k)
-                    quant_tok(2 * k + 1)
                 if n in QF_EARLY:
                     quant_feat(SEQ[n - 1], 0)
                     quant_feat(SEQ[n - 1], 1)
@@ -493,11 +497,8 @@ def tile_dbrxattention_pa_v_kernel(
             if n > 0:
                 p = SEQ[n - 1]
                 if all(q in SEQ[:n] for q in (p % 3, p % 3 + 3)):
-                    for h in range(2 if p % 3 == 2 else 4):
-                        out1_row(2 * (p % 3) + h // 2, h % 2, EV[n][2 * h : 2 * h + 2])
-                if n == 4:
-                    out1_row(5, 0, "ss")
-                    out1_row(5, 1, "ss")
+                    for h in range(4):
+                        out1_row(p % 3, h, EV[n][2 * h : 2 * h + 2])
                 g = p // 3
                 if all(q in SEQ[:n] for q in (3 * g, 3 * g + 1, 3 * g + 2)):
                     for j in range(4):
@@ -510,7 +511,6 @@ def tile_dbrxattention_pa_v_kernel(
                     out0_open(k // 3, j)
                 step_add(k, 0, 2)
                 step_add(k, 2, 4)
-                quant_tok(2 * k)
             else:
                 step_add(k, 0, 2 if v_unit else 4)
                 g = SEQ[n + 1] // 3
@@ -526,27 +526,25 @@ def tile_dbrxattention_pa_v_kernel(
                 for c, e in fills:
                     if not (e == "s" and c in LATE):
                         fill_quant(ch_of(c))
-                quant_tok(2 * k)
-                if n == 0 or not v_unit:
-                    quant_tok(2 * k + 1)
-                transposes(k, 0, "ss")
-                transposes(k, 1, "ss")
+                quant_tok(k)
+                transposes(k, 0, "s")
+                transposes(k, 1, "s")
         k = SEQ[5]
         g = k // 3
-        transposes(k, 0, "sv")
-        quant_tok(2 * k + 1)
+        transposes(k, 0, "s")
+        quant_tok(k)
         quant_feat(k, 0)
-        transposes(k, 1, "sv")
+        transposes(k, 1, "v")
         quant_feat(k, 1)
         e = 0
         for h in range(2):
-            out1_row((2 * k) % 6, h, EV_TAIL[e : e + 2])
+            out1_row(k % 3, h, EV_TAIL[e : e + 2])
             e += 2
         for j in range(NOPEN):
             out0_close(g, j, EV_TAIL[e : e + 2])
             e += 2
         for h in range(2):
-            out1_row((2 * k + 1) % 6, h, EV_TAIL[e : e + 2])
+            out1_row(k % 3, 2 + h, EV_TAIL[e : e + 2])
             e += 2
         for j in range(NOPEN, 4):
             out0_row(g, j, EV_TAIL[e : e + 2])

import math
from contextlib import ExitStack

import concourse.mybir as mybir
from concourse.masks import make_identity

T, D, O = 1024, 1024, 1536
HD = 128
ROPE_BASE = 500000.0
CLAMP = 8.0
FLOPS = 2 * 2 * T * D * O

F32 = mybir.dt.float32
BF16 = mybir.dt.bfloat16
I32 = mybir.dt.int32
U32 = mybir.dt.uint32
U8 = mybir.dt.uint8
E4M3 = mybir.dt.float8_e4m3fn_x4
E5M2 = mybir.dt.float8_e5m2_x4
ALU = mybir.AluOpType
ACT = mybir.ActivationFunctionType

P = 128
SEQ = (2, 0, 1, 3, 5, 4)
SEQ_G = (0, 2, 1)
LOADS = (5, 4, 0, "w2", 1, 2, 3, "w0", "w1", 6, 7, "x0", "x1", 11, 10, 8, 9)
FILLS = {
    0: (("w20", "s"),),
    1: (("w00", "s"), ("w01", "s"), ("w21", "g")),
    2: (("w11", "s"), ("x00", "s"), ("w10", "g")),
    3: (("x10", "s"), ("x01", "g"), ("x11", "s")),
}
LATE = ("w20", "w01", "x00", "x11")
EV = {1: "ssssssss", 2: "ssssssss", 3: "ssssssss", 4: "ssssssss", 5: "ssssssss", 6: "ssss"}
QF_EARLY = (3,)
ABS_AFTER = ()
EV_TAIL = "sssvsvsvsvsvsvsvsvsvsv"
NOPEN = 0


def tile_dbrxattention_pa_v_kernel(
    tc, x, w_qkv, q_rot, k_rot, v_pre, grad_0, grad_1, grad_2, out_0, out_1
):
    nc = tc.nc
    with ExitStack() as ctx:
        const = ctx.enter_context(tc.tile_pool(name="const", bufs=1))
        keep = ctx.enter_context(tc.tile_pool(name="keep", bufs=1))
        pq = ctx.enter_context(tc.tile_pool(name="pq", bufs=3))
        pg = ctx.enter_context(tc.tile_pool(name="pg", bufs=4))
        praw = ctx.enter_context(tc.tile_pool(name="praw", bufs=4))
        pil = ctx.enter_context(tc.tile_pool(name="pil", bufs=4))
        work1 = ctx.enter_context(tc.tile_pool(name="work1", bufs=1))
        work2 = ctx.enter_context(tc.tile_pool(name="work2", bufs=2))
        pst = ctx.enter_context(tc.tile_pool(name="pst", bufs=6))
        ptp = ctx.enter_context(tc.psum_pool(name="ptp", bufs=2))
        pacc = ctx.enter_context(tc.psum_pool(name="pacc", bufs=6))
        ctx.enter_context(tc.manual_schedule())

        qt = {}
        gt = {}
        raw = {}

        def load_unit(u):
            g, pr = divmod(u, 6)
            rows = slice(512 * g, 512 * g + 512)
            if pr < 4:
                sv = q_rot[0, 2 * pr : 2 * pr + 2, rows, :]
                gr = grad_0[0, 2 * pr : 2 * pr + 2, rows, :]
            elif pr == 4:
                sv = k_rot[0, :, rows, :]
                gr = grad_1[0, :, rows, :]
            else:
                sv = v_pre[0, :, rows, :]
                gr = grad_2[0, :, rows, :]
            k, s = divmod(u, 2)
            if k not in qt:
                q_t = pq.tile([P, 4, 512], F32, name="q_t")
                g_t = pg.tile([P, 4, 512], BF16, name="g_t")
                qt[k] = q_t
                gt[k] = g_t
            hs = slice(2 * s, 2 * s + 2)
            nc.sync.dma_start(out=qt[k][:, hs, :], in_=sv.rearrange("h (p j) c -> p h (j c)", j=4))
            nc.sync.dma_start(out=gt[k][:, hs, :], in_=gr.rearrange("h (p j) c -> p h (j c)", j=4))

        def load_w(i):
            r = praw.tile([P, 4, 1024], BF16, name="raw_t")
            nc.sync.dma_start(
                out=r[:], in_=w_qkv[512 * i : 512 * i + 512, :].rearrange("(p j) d -> p j d", j=4)
            )
            raw["w", i] = r

        def load_x(i):
            r = praw.tile([P, 4, 1024], BF16, name="raw_t")
            nc.sync.dma_start(
                out=r[:], in_=x[0, 512 * i : 512 * i + 512, :].rearrange("(p j) d -> p j d", j=4)
            )
            raw["x", i] = r

        def do_load(ld):
            if isinstance(ld, int):
                load_unit(ld)
            elif ld[0] == "w":
                load_w(int(ld[1]))
            else:
                load_x(int(ld[1]))

        for ld in LOADS[:4]:
            do_load(ld)

        ones = const.tile([P, 1], F32, name="ones")
        nc.vector.memset(ones[:], 1.0)
        sgn = const.tile([P, 2], F32, name="sgn")
        nc.vector.memset(sgn[:, 0:1], 1.0)
        nc.vector.memset(sgn[:, 1:2], -1.0)
        ident_f = const.tile([P, P], F32, name="ident_f")
        make_identity(nc, ident_f[:])
        tok = const.tile([P, 512], F32, name="tok")
        nc.gpsimd.iota(
            tok[:].rearrange("p (j n) -> p j n", j=4),
            [[1, 4], [4, 128]],
            base=0,
            channel_multiplier=0,
            allow_small_or_imprecise_dtypes=True,
        )
        warm = const.tile([P, 1], F32, name="warm")
        nc.scalar.activation(warm[:], ones[:], ACT.Sin)

        ca = const.tile([P, 8], F32, name="ca")
        cb = const.tile([P, 8], F32, name="cb")
        for i in range(8):
            nc.vector.tensor_scalar_mul(cb[:, i : i + 1], ones[:], ROPE_BASE ** (-2.0 * i / HD))
            nc.scalar.activation(
                ca[:, i : i + 1], ones[:], ACT.Copy, scale=ROPE_BASE ** (-16.0 * i / HD) / (2.0 * math.pi)
            )
        cbs = const.tile([P, 8, 2], F32, name="cbs")
        nc.vector.tensor_tensor(
            out=cbs[:],
            in0=cb[:].unsqueeze(2).to_broadcast([P, 8, 2]),
            in1=sgn[:].unsqueeze(1).to_broadcast([P, 8, 2]),
            op=ALU.mult,
        )
        row = const.tile([P, 8, 16], F32, name="row")
        nc.vector.tensor_tensor(
            out=row[:],
            in0=ca[:].unsqueeze(2).to_broadcast([P, 8, 16]),
            in1=cbs[:].rearrange("p b e -> p (b e)").unsqueeze(1).to_broadcast([P, 8, 16]),
            op=ALU.mult,
        )
        col_p = ptp.tile([P, P], F32, name="tp_t")
        nc.tensor.transpose(col_p[:], row[:].rearrange("p a b -> p (a b)"), ident_f[:])
        col = const.tile([P, 1], F32, name="col")
        nc.vector.tensor_copy(out=col[:], in_=col_p[:, 0:1])

        cos_p = {}
        sin_p = {}
        sin_s = {}
        fr = {}

        def turns(g):
            y = const.tile([P, 512], F32, name="y_t")
            nc.vector.tensor_scalar(
                out=y[:], in0=tok[:], scalar1=512.0 * g, scalar2=col[:], op0=ALU.add, op1=ALU.mult
            )
            n_i = const.tile([P, 512], I32, name="n_t")
            nc.vector.tensor_copy(out=n_i[:], in_=y[:])
            f = const.tile([P, 512], F32, name="f_t")
            nc.vector.tensor_tensor(out=f[:], in0=y[:], in1=n_i[:], op=ALU.subtract)
            fr[g] = f

        def trig(g):
            f = fr[g]
            fa = const.tile([P, 512], F32, name="n_t")
            nc.scalar.activation(fa[:], f[:], ACT.Abs)
            sv = const.tile([P, 512], F32, name=f"sv{g}")
            nc.scalar.activation(sv[:], f[:], ACT.Sin, scale=2.0 * math.pi)
            fc = const.tile([P, 512], F32, name="y_t")
            nc.vector.tensor_scalar(
                out=fc[:], in0=fa[:], scalar1=-1.0, scalar2=0.25, op0=ALU.mult, op1=ALU.add
            )
            cv = const.tile([P, 512], F32, name=f"cv{g}")
            nc.scalar.activation(cv[:], fc[:], ACT.Sin, scale=2.0 * math.pi)
            return sv, cv

        def tables_p(g, sv, cv):
            cp = pacc.tile([P, 4, P], F32, name="acc_t")
            for j in range(4):
                nc.tensor.transpose(cp[:, j, :], cv[:, P * j : P * j + P], ident_f[:])
            sp = pacc.tile([P, 4, P], F32, name="acc_t")
            for j in range(4):
                nc.tensor.transpose(sp[:, j, :], sv[:, P * j : P * j + P], ident_f[:])
            cos_p[g] = cp
            sin_p[g] = sp

        def tables_s(g):
            ss = const.tile([P, 4, P], F32, name=f"sin_s{g}")
            nc.scalar.copy(out=ss[:], in_=sin_p[g][:])
            sin_s[g] = ss

        ha = {}
        mk = {}
        gm = {}
        t1 = {}
        t2 = {}
        dq = {}

        def step_abs(u):
            k, s = divmod(u, 2)
            if k not in ha:
                a = work2.tile([P, 4, 512], BF16, name="ha_t")
                ha[k] = a
            hs = slice(2 * s, 2 * s + 2)
            top = (
                qt[k][:, hs, :]
                .rearrange("p h n -> p (h n)")
                .bitcast(BF16)
                .rearrange("p (n e) -> p n e", e=2)[:, :, 1]
            )
            nc.scalar.activation(ha[k][:, hs, :].rearrange("p h n -> p (h n)"), top, ACT.Abs)

        def new_group(k):
            m = work1.tile([P, 4, 512], BF16, name="mk_t")
            mk[k] = m
            d_t = work2.tile([P, 4, P, 4], BF16, name="dq_t", align_bytes=64)
            dq[k] = d_t
            nh = 2 if k % 3 == 2 else 4
            g_m = work1.tile([P, nh, 4, 64, 2], BF16, name="gm_t")
            gm[k] = g_m
            a = work1.tile([P, 4, nh, P], F32, name="t1_t")
            t1[k] = a
            b = work1.tile([P, 4, nh, P], F32, name="t2_t")
            t2[k] = b

        def step_cmp(k, h0, h1):
            nc.vector.tensor_scalar(
                out=mk[k][:, h0:h1, :].rearrange("p h n -> p (h n)"),
                in0=ha[k][:, h0:h1, :].rearrange("p h n -> p (h n)"),
                scalar1=CLAMP,
                scalar2=None,
                op0=ALU.is_lt,
            )

        def step_mask_v(k):
            for h in range(2, 4):
                nc.vector.tensor_tensor(
                    out=dq[k][:, :, 32 * h : 32 * h + 32, :].rearrange("p t q j -> p q j t"),
                    in0=mk[k][:, h, :].rearrange("p (j q t) -> p q j t", j=4, t=4),
                    in1=gt[k][:, h, :].rearrange("p (j q t) -> p q j t", j=4, t=4),
                    op=ALU.mult,
                )

        def step_mask(k, h0, h1):
            nc.vector.tensor_tensor(
                out=gm[k][:, h0:h1].rearrange("p h j i e -> p (h j i e)"),
                in0=mk[k][:, h0:h1, :].rearrange("p h n -> p (h n)"),
                in1=gt[k][:, h0:h1, :].rearrange("p h n -> p (h n)"),
                op=ALU.mult,
            )

        def step_cos(k, h0, h1):
            nc.vector.tensor_tensor(
                out=t1[k][:, :, h0:h1, :].rearrange("p j h c -> p h j c"),
                in0=gm[k][:, h0:h1].rearrange("p h j i e -> p h j (i e)"),
                in1=cos_p[k // 3][:].unsqueeze(1).to_broadcast([P, h1 - h0, 4, P]),
                op=ALU.mult,
            )

        def step_sin(k, h0, h1, eng):
            tab = sin_p[k // 3] if eng == "v" else sin_s[k // 3]
            e = nc.vector if eng == "v" else nc.gpsimd
            e.tensor_tensor(
                out=t2[k][:, :, h0:h1, :].rearrange("p j h (i e) -> p h j i e", e=2),
                in0=gm[k][:, h0:h1, :, :, ::-1],
                in1=tab[:]
                .rearrange("p j (i e) -> p j i e", e=2)
                .unsqueeze(1)
                .to_broadcast([P, h1 - h0, 4, 64, 2]),
                op=ALU.mult,
            )

        def step_add(k, h0, h1):
            nc.vector.tensor_tensor(
                out=dq[k][:, :, 32 * h0 : 32 * h1, :].rearrange("p t q j -> p q j t"),
                in0=t1[k][:, :, h0:h1, :].rearrange("p j h (q t) -> p (h q) j t", t=4),
                in1=t2[k][:, :, h0:h1, :].rearrange("p j h (q t) -> p (h q) j t", t=4),
                op=ALU.add,
            )

        tokc = {}
        toks = {}
        featc = {}
        feats = {}

        def quant_tok(k):
            c = keep.tile([P, 512], U32, name=f"tokc{k}", align_bytes=64)
            s = keep.tile([P, 512], U8, name=f"toks{k}", align_bytes=64)
            nc.vector.quantize_mx(
                out=c[:].bitcast(E5M2), scales=s[:], in_=dq[k][:].rearrange("p t q j -> p (t q j)")
            )
            tokc[k] = c
            toks[k] = s

        dqt = {}

        def transposes(k, half, eng):
            o = work2.tile([P, 2, P, 4], BF16, name=f"dqt{half}", align_bytes=64)
            pairs = (
                dq[k][:]
                .rearrange("p t q j -> p (t q j)")
                .bitcast(F32)
                .rearrange("p (t q w) -> p t q w", t=4, w=2)
            )
            tp = ptp.tile([P, 4, P], F32, name="tp_t")
            for t in range(4):
                nc.tensor.transpose(tp[:, t, :], pairs[:, t, :, half], ident_f[:])
            src = (
                tp[:]
                .rearrange("p t n -> p (t n)")
                .bitcast(BF16)
                .rearrange("p (t n e) -> p e n t", t=4, e=2)
            )
            if eng == "s":
                nc.scalar.copy(out=o[:], in_=src)
            else:
                nc.vector.tensor_copy(out=o[:], in_=src)
            dqt[k, half] = o

        def quant_feat(k, half):
            c = keep.tile([P, 256], U32, name=f"featc{k}{half}", align_bytes=64)
            s = keep.tile([P, 256], U8, name=f"feats{k}{half}", align_bytes=64)
            nc.vector.quantize_mx(
                out=c[:].bitcast(E5M2),
                scales=s[:],
                in_=dqt[k, half][:].rearrange("p j n t -> p (j n t)"),
            )
            featc[k, half] = c
            feats[k, half] = s

        inter = {}
        chc = {}
        chs = {}

        def fill_copy(ch, eng):
            kind, i, h = ch
            o = pil.tile([P, 512, 4], BF16, name="il_t", align_bytes=64)
            dst = o[:].rearrange("p (c i) t -> p c t i", i=4)
            src = raw[kind, i][:, :, 512 * h : 512 * h + 512].rearrange("p t (c i) -> p c t i", i=4)
            if eng == "g":
                nc.gpsimd.tensor_scalar(
                    out=o[:],
                    in0=raw[kind, i][:, :, 512 * h : 512 * h + 512].rearrange("p t c -> p c t"),
                    scalar1=1.0,
                    scalar2=0.0,
                    op0=ALU.mult,
                    op1=ALU.add,
                )
            elif eng == "s":
                nc.scalar.copy(out=dst, in_=src)
            else:
                nc.vector.tensor_copy(out=dst, in_=src)
            inter[ch] = o

        def fill_quant(ch):
            kind, i, h = ch
            c = keep.tile([P, 512], U32, name=f"c{kind}{i}{h}", align_bytes=64)
            s = keep.tile([P, 512], U8, name=f"s{kind}{i}{h}", align_bytes=64)
            nc.vector.quantize_mx(
                out=c[:].bitcast(E4M3), scales=s[:], in_=inter[ch][:].rearrange("p n t -> p (n t)")
            )
            chc[ch] = c
            chs[ch] = s

        def passes(acc, lhs, kind, h, lo, hi):
            for n in range(lo, hi):
                c, s, cols = lhs[n]
                nc.tensor.matmul_mx(
                    out=acc[:],
                    lhsT=c[:, cols].bitcast(E5M2),
                    lhsT_scale=s[:, cols],
                    rhs=chc[kind, SEQ_G[n] if kind == "w" else n, h][:].bitcast(E4M3),
                    rhs_scale=chs[kind, SEQ_G[n] if kind == "w" else n, h][:],
                    start=(n == 0),
                    stop=(n == len(lhs) - 1),
                )

        def evac(st, acc, h, eng):
            if eng == "s":
                nc.scalar.copy(out=st[:, 512 * h : 512 * h + 512], in_=acc[:])
            else:
                nc.vector.tensor_copy(out=st[:, 512 * h : 512 * h + 512], in_=acc[:])

        def lhs0(g, j, n):
            kk = 3 * g + SEQ_G[n]
            return featc[kk, j // 2], feats[kk, j // 2], slice(P * (j % 2), P * (j % 2) + P)

        def out0_row(g, j, engines):
            dst = out_0[0, 512 * g : 512 * g + 512, :].rearrange("(p j) d -> j p d", j=4)[j]
            st = pst.tile([P, 1024], F32, name="st_t")
            lhs = [lhs0(g, j, n) for n in range(3)]
            for h in range(2):
                acc = pacc.tile([P, 512], F32, name="acc_t")
                passes(acc, lhs, "w", h, 0, 3)
                evac(st, acc, h, engines[h])
            nc.sync.dma_start(out=dst, in_=st[:])

        early = {}

        def out0_open(g, j):
            lhs = [lhs0(g, j, n) for n in range(2)] + [None]
            for h in range(2):
                acc = pacc.tile([P, 512], F32, name="acc_t")
                passes(acc, lhs, "w", h, 0, 2)
                early[g, j, h] = acc

        def out0_close(g, j, engines):
            dst = out_0[0, 512 * g : 512 * g + 512, :].rearrange("(p j) d -> j p d", j=4)[j]
            st = pst.tile([P, 1024], F32, name="st_t")
            lhs = [None, None, lhs0(g, j, 2)]
            for h in range(2):
                passes(early[g, j, h], lhs, "w", h, 2, 3)
                evac(st, early[g, j, h], h, engines[h])
            nc.sync.dma_start(out=dst, in_=st[:])

        def out1_row(grp, t, engines):
            dst = out_1[512 * grp : 512 * grp + 512, :].rearrange("(p t) d -> t p d", t=4)[t]
            st = pst.tile([P, 1024], F32, name="st_t")
            cols = slice(P * t, P * t + P)
            lhs = [(tokc[3 * g + grp], toks[3 * g + grp], cols) for g in range(2)]
            for hh in range(2):
                acc = pacc.tile([P, 512], F32, name="acc_t")
                passes(acc, lhs, "x", hh, 0, 2)
                evac(st, acc, hh, engines[hh])
            nc.sync.dma_start(out=dst, in_=st[:])

        def ch_of(c):
            return c[0], int(c[1]), int(c[2])

        g_first = SEQ[0] // 3
        k0 = SEQ[0]
        new_group(k0)
        turns(g_first)
        step_abs(2 * k0 + 1)
        step_cmp(k0, 2, 4)
        tabs = {}
        tabs[g_first] = trig(g_first)
        step_abs(2 * k0)
        step_mask_v(k0)
        tables_p(g_first, *tabs[g_first])
        tables_s(g_first)
        step_cmp(k0, 0, 2)
        turns(1 - g_first)
        for ld in LOADS[4:]:
            do_load(ld)
        for n in range(6):
            k = SEQ[n]
            v_unit = k % 3 == 2
            last = n == 5
            fills = FILLS.get(n, ())
            gf = [c for c, e in fills if e == "g"]
            if v_unit:
                if n > 0:
                    step_mask_v(k)
                if n in QF_EARLY:
                    quant_feat(SEQ[n - 1], 0)
                    quant_feat(SEQ[n - 1], 1)
                step_mask(k, 0, 2)
                step_cos(k, 0, 2)
                step_sin(k, 1, 2, "g")
                step_sin(k, 0, 1, "v")
            else:
                step_mask(k, 0, 2)
                if n in QF_EARLY:
                    quant_feat(SEQ[n - 1], 0)
                    quant_feat(SEQ[n - 1], 1)
                step_mask(k, 2, 4)
                step_cos(k, 0, 4)
                if gf:
                    step_sin(k, 3, 4, "g")
                    fill_copy(ch_of(gf[0]), "g")
                    step_sin(k, 0, 3, "v")
                else:
                    step_sin(k, 2, 4, "g")
                    step_sin(k, 0, 2, "v")
            if not last and n not in ABS_AFTER:
                step_abs(2 * SEQ[n + 1])
                step_abs(2 * SEQ[n + 1] + 1)
            if n > 0 and n not in QF_EARLY:
                quant_feat(SEQ[n - 1], 0)
                quant_feat(SEQ[n - 1], 1)
            for c, e in FILLS.get(n - 1, ()):
                if e == "s" and c in LATE:
                    fill_quant(ch_of(c))
            if n == 0:
                tabs[1 - g_first] = trig(1 - g_first)
            for c, e in fills:
                if e == "s":
                    fill_copy(ch_of(c), "s")
            if n > 0:
                p = SEQ[n - 1]
                if all(q in SEQ[:n] for q in (p % 3, p % 3 + 3)):
                    for h in range(4):
                        out1_row(p % 3, h, EV[n][2 * h : 2 * h + 2])
                g = p // 3
                if all(q in SEQ[:n] for q in (3 * g, 3 * g + 1, 3 * g + 2)):
                    for j in range(4):
                        out0_row(g, j, EV[n][2 * j : 2 * j + 2])
            if not last and n in ABS_AFTER:
                step_abs(2 * SEQ[n + 1])
                step_abs(2 * SEQ[n + 1] + 1)
            if last:
                for j in range(NOPEN):
                    out0_open(k // 3, j)
                step_add(k, 0, 2)
                step_add(k, 2, 4)
            else:
                step_add(k, 0, 2 if v_unit else 4)
                g = SEQ[n + 1] // 3
                if g != k // 3:
                    tables_p(g, *tabs[g])
                    if g not in sin_s:
                        tables_s(g)
                new_group(SEQ[n + 1])
                step_cmp(SEQ[n + 1], 0, 4)
                for c, e in fills:
                    if e == "v":
                        fill_copy(ch_of(c), "v")
                for c, e in fills:
                    if not (e == "s" and c in LATE):
                        fill_quant(ch_of(c))
                quant_tok(k)
                transposes(k, 0, "s")
                transposes(k, 1, "s")
        k = SEQ[5]
        g = k // 3
        transposes(k, 0, "s")
        quant_tok(k)
        quant_feat(k, 0)
        transposes(k, 1, "v")
        quant_feat(k, 1)
        e = 0
        for h in range(2):
            out1_row(k % 3, h, EV_TAIL[e : e + 2])
            e += 2
        for j in range(NOPEN):
            out0_close(g, j, EV_TAIL[e : e + 2])
            e += 2
        for h in range(2):
            out1_row(k % 3, 2 + h, EV_TAIL[e : e + 2])
            e += 2
        for j in range(NOPEN, 4):
            out0_row(g, j, EV_TAIL[e : e + 2])
            e += 2
